import numpy as np
import ml_dtypes


def mxq(x, axis, fmt="e4m3"):
    dtype, down = {"e4m3": (ml_dtypes.float8_e4m3fn, 7), "e5m2": (ml_dtypes.float8_e5m2, 14)}[fmt]
    v = np.moveaxis(np.asarray(x, np.float32).astype(ml_dtypes.bfloat16).astype(np.float64), axis, -1)
    blocks = v.reshape(v.shape[:-1] + (-1, 32))
    amax = np.abs(blocks).max(-1, keepdims=True)
    byte = np.maximum(np.where(amax > 0, np.frexp(amax)[1] - 1 + 127, 0) - down, 1)
    scale = np.exp2(byte - 127.0)
    codes = (blocks / scale).astype(np.float32).astype(dtype).astype(np.float64)
    return np.moveaxis((codes * scale).reshape(v.shape), -1, axis)


WIDE = False


def mx_kscale(k):
    if not WIDE:
        return np.ones(k)
    levels = np.array([20, -20, 10, -10, 0])
    a = np.random.permutation(np.resize(levels, k // 512 * 4)).reshape(k // 512, 4)
    idx = np.arange(k)
    return np.exp2(a[idx // 512, idx % 128 // 32])


BF16 = ml_dtypes.bfloat16


def bf(x):
    return np.asarray(x, np.float32).astype(BF16)


def f64(x):
    return np.asarray(x).astype(np.float64)


B, F, O = 1024, 2048, 1024


def setup_inputs():
    s = mx_kscale(B)
    x = np.random.standard_normal((B, 2, F)) * s[:, None, None]
    fr = np.random.standard_normal((O, F)) * 0.5 / np.sqrt(F)
    fi = np.random.standard_normal((O, F)) * 0.5 / np.sqrt(F)
    g = np.random.standard_normal((B, O)) * np.exp2(np.random.randint(-12, 1, (B, 1))) / s[:, None]
    return {"x": bf(x), "filters_real": bf(fr), "filters_imag": bf(fi), "grad_out": bf(g)}


def reference(x, filters_real, filters_imag, grad_out):
    x = f64(x)
    gq = mxq(f64(grad_out), 0, "e5m2")
    d_wr = gq.T @ mxq(x[:, 0], 0, "e4m3")
    d_wi = gq.T @ mxq(x[:, 1], 0, "e4m3")
    return d_wr + d_wi

@@ -1,0 +1,144 @@
+from contextlib import ExitStack
+
+import concourse.mybir as mybir
+
+BF16 = mybir.dt.bfloat16
+F32 = mybir.dt.float32
+U32 = mybir.dt.uint32
+U8 = mybir.dt.uint8
+E4M3X4 = mybir.dt.float8_e4m3fn_x4
+E5M2X4 = mybir.dt.float8_e5m2_x4
+
+P = 128
+PACK = 4
+TOKENS = 1024
+FEAT = 2048
+OUTF = 1024
+W = 512
+N_C = TOKENS // (P * PACK)
+N_S = FEAT // W
+N_M = OUTF // P
+V_COLS = 320
+GRP_BUFS = 6
+
+FLOPS = 2 * 2 * TOKENS * OUTF * FEAT
+BYTES = 2 * TOKENS * 2 * FEAT + 2 * TOKENS * OUTF + 4 * OUTF * FEAT
+
+
+def tile_fftmlp_kernel(tc, x, filters_real, filters_imag, grad_out, out):
+    nc = tc.nc
+    xv = x.rearrange("(c p j) h f -> c h p j f", c=N_C, p=P, j=PACK)
+    gv = grad_out.rearrange("(c p j) o -> c p j o", c=N_C, p=P, j=PACK)
+
+    head = []
+    for c in range(N_C):
+        for h in range(2):
+            head.append(("g", c, h, 0))
+            head.append(("x", c, h, 0))
+    rest = [("x", c, h, s) for s in range(1, N_S) for c in range(N_C) for h in range(2)]
+    units = head + rest
+
+    with ExitStack() as ctx:
+        raw_pool = ctx.enter_context(tc.tile_pool(name="raw", bufs=1))
+        grp_pool = ctx.enter_context(tc.tile_pool(name="grp", bufs=GRP_BUFS))
+        mx_pool = ctx.enter_context(tc.tile_pool(name="mx", bufs=1))
+        res_pool = ctx.enter_context(tc.tile_pool(name="res", bufs=N_M * N_S))
+        psum = ctx.enter_context(tc.psum_pool(name="acc", bufs=8))
+        ctx.enter_context(tc.manual_schedule())
+
+        raws = {}
+        codes = {}
+        scales = {}
+        groups = {}
+
+        for u in units:
+            kind, c, h, s = u
+            label = "%s%d%d%d" % u
+            raw = raw_pool.tile([P, PACK, W], BF16, name="raw" + label)
+            if kind == "g":
+                src = gv[c, :, :, h * W:(h + 1) * W]
+            else:
+                src = xv[c, h, :, :, s * W:(s + 1) * W]
+            nc.sync.dma_start(out=raw[:], in_=src)
+            raws[u] = raw
+
+        def regroup(copy, u, lo, hi):
+            copy(
+                out=groups[u][:, lo:hi, :].rearrange("p (q i) t -> p q t i", i=4),
+                in_=raws[u][:, :, lo:hi].rearrange("p t (q i) -> p q t i", i=4),
+            )
+
+        def new_group(u):
+            grouped = grp_pool.tile([P, W, PACK], BF16, name="grouped", align_bytes=64)
+            groups[u] = grouped
+
+        def quantise(u):
+            label = "%s%d%d%d" % u
+            cod = mx_pool.tile([P, W], U32, name="cod" + label, align_bytes=64)
+            scl = mx_pool.tile([P, W], U8, name="scl" + label, align_bytes=64)
+            fmt = E5M2X4 if u[0] == "g" else E4M3X4
+            nc.vector.quantize_mx(
+                out=cod[:].bitcast(fmt),
+                scales=scl[:],
+                in_=groups[u][:].rearrange("p w t -> p (w t)"),
+            )
+            codes[u] = cod
+            scales[u] = scl
+
+        for u in head:
+            new_group(u)
+            regroup(nc.vector.tensor_copy, u, 0, V_COLS)
+            regroup(nc.scalar.copy, u, V_COLS, W)
+            quantise(u)
+        for i, u in enumerate(rest):
+            new_group(u)
+            regroup(nc.vector.tensor_copy, u, 0, W)
+            if i > 0:
+                quantise(rest[i - 1])
+        quantise(rest[-1])
+
+        def mx_pass(acc, m, c, h, s, start, stop):
+            gu = ("g", c, m // 4, 0)
+            xu = ("x", c, h, s)
+            cols = slice((m % 4) * P, (m % 4 + 1) * P)
+            nc.tensor.matmul_mx(
+                out=acc[:],
+                lhsT=codes[gu][:, cols].bitcast(E5M2X4),
+                lhsT_scale=scales[gu][:, cols],
+                rhs=codes[xu][:].bitcast(E4M3X4),
+                rhs_scale=scales[xu][:],
+                start=start,
+                stop=stop,
+            )
+
+        def drain(copy, acc, m, s):
+            res = res_pool.tile([P, W], F32, name="res")
+            copy(out=res[:], in_=acc[:])
+            nc.sync.dma_start(out=out[m * P:(m + 1) * P, s * W:(s + 1) * W], in_=res[:])
+
+        for s in range(N_S):
+            banks = []
+            for m in range(N_M):
+                acc = psum.tile([P, W], F32, name="acc")
+                banks.append(acc)
+            if s == 0:
+                for c in range(N_C):
+                    for h in range(2):
+                        for m in range(N_M):
+                            mx_pass(banks[m], m, c, h, s, c == 0 and h == 0, c == 1 and h == 1)
+                for m in range(N_M):
+                    drain(nc.scalar.copy, banks[m], m, s)
+            elif s < N_S - 1:
+                for h in range(2):
+                    for m in range(N_M):
+                        mx_pass(banks[m], m, 0, h, s, h == 0, False)
+                for m in range(N_M):
+                    mx_pass(banks[m], m, 1, 0, s, False, False)
+                    mx_pass(banks[m], m, 1, 1, s, False, True)
+                    drain(nc.scalar.copy, banks[m], m, s)
+            else:
+                for m in range(N_M):
+                    for c in range(N_C):
+                        for h in range(2):
+                            mx_pass(banks[m], m, c, h, s, c == 0 and h == 0, c == 1 and h == 1)
+                    drain(nc.vector.tensor_copy if m % 2 else nc.scalar.copy, banks[m], m, s)

@@ -20,6 +20,7 @@ N_S = FEAT // W
 N_M = OUTF // P
 V_COLS = 320
 GRP_BUFS = 6
+N_SHARE = 12
 
 FLOPS = 2 * 2 * TOKENS * OUTF * FEAT
 BYTES = 2 * TOKENS * 2 * FEAT + 2 * TOKENS * OUTF + 4 * OUTF * FEAT
@@ -44,7 +45,6 @@ def tile_fftmlp_kernel(tc, x, filters_real, filters_imag, grad_out, out):
         mx_pool = ctx.enter_context(tc.tile_pool(name="mx", bufs=1))
         res_pool = ctx.enter_context(tc.tile_pool(name="res", bufs=N_M * N_S))
         psum = ctx.enter_context(tc.psum_pool(name="acc", bufs=8))
-        ctx.enter_context(tc.manual_schedule())
 
         raws = {}
         codes = {}
@@ -85,17 +85,14 @@ def tile_fftmlp_kernel(tc, x, filters_real, filters_imag, grad_out, out):
             codes[u] = cod
             scales[u] = scl
 
-        for u in head:
+        for i, u in enumerate(units):
             new_group(u)
-            regroup(nc.vector.tensor_copy, u, 0, V_COLS)
-            regroup(nc.scalar.copy, u, V_COLS, W)
+            if i < N_SHARE:
+                regroup(nc.vector.tensor_copy, u, 0, V_COLS)
+                regroup(nc.scalar.copy, u, V_COLS, W)
+            else:
+                regroup(nc.vector.tensor_copy, u, 0, W)
             quantise(u)
-        for i, u in enumerate(rest):
-            new_group(u)
-            regroup(nc.vector.tensor_copy, u, 0, W)
-            if i > 0:
-                quantise(rest[i - 1])
-        quantise(rest[-1])
 
         def mx_pass(acc, m, c, h, s, start, stop):
             gu = ("g", c, m // 4, 0)
@@ -117,28 +114,9 @@ def tile_fftmlp_kernel(tc, x, filters_real, filters_imag, grad_out, out):
             nc.sync.dma_start(out=out[m * P:(m + 1) * P, s * W:(s + 1) * W], in_=res[:])
 
         for s in range(N_S):
-            banks = []
             for m in range(N_M):
                 acc = psum.tile([P, W], F32, name="acc")
-                banks.append(acc)
-            if s == 0:
                 for c in range(N_C):
                     for h in range(2):
-                        for m in range(N_M):
-                            mx_pass(banks[m], m, c, h, s, c == 0 and h == 0, c == 1 and h == 1)
-                for m in range(N_M):
-                    drain(nc.scalar.copy, banks[m], m, s)
-            elif s < N_S - 1:
-                for h in range(2):
-                    for m in range(N_M):
-                        mx_pass(banks[m], m, 0, h, s, h == 0, False)
-                for m in range(N_M):
-                    mx_pass(banks[m], m, 1, 0, s, False, False)
-                    mx_pass(banks[m], m, 1, 1, s, False, True)
-                    drain(nc.scalar.copy, banks[m], m, s)
-            else:
-                for m in range(N_M):
-                    for c in range(N_C):
-                        for h in range(2):
-                            mx_pass(banks[m], m, c, h, s, c == 0 and h == 0, c == 1 and h == 1)
-                    drain(nc.vector.tensor_copy if m % 2 else nc.scalar.copy, banks[m], m, s)
+                        mx_pass(acc, m, c, h, s, c == 0 and h == 0, c == 1 and h == 1)
+                drain(nc.scalar.copy, acc, m, s)

@@ -19,8 +19,10 @@ N_C = TOKENS // (P * PACK)
 N_S = FEAT // W
 N_M = OUTF // P
 V_COLS = 320
-GRP_BUFS = 6
+V_COLS_LATE = 512
 N_SHARE = 12
+GRP_BUFS = 6
+PINNED = False
 
 FLOPS = 2 * 2 * TOKENS * OUTF * FEAT
 BYTES = 2 * TOKENS * 2 * FEAT + 2 * TOKENS * OUTF + 4 * OUTF * FEAT
@@ -31,20 +33,27 @@ def tile_fftmlp_kernel(tc, x, filters_real, filters_imag, grad_out, out):
     xv = x.rearrange("(c p j) h f -> c h p j f", c=N_C, p=P, j=PACK)
     gv = grad_out.rearrange("(c p j) o -> c p j o", c=N_C, p=P, j=PACK)
 
-    head = []
+    units = []
     for c in range(N_C):
         for h in range(2):
-            head.append(("g", c, h, 0))
-            head.append(("x", c, h, 0))
-    rest = [("x", c, h, s) for s in range(1, N_S) for c in range(N_C) for h in range(2)]
-    units = head + rest
+            units.append(("g", c, h, 0))
+            units.append(("x", c, h, 0))
+    for c in range(N_C):
+        for h in range(2):
+            units.append(("x", c, h, 1))
+    for c in range(N_C):
+        for h in range(2):
+            units.append(("x", c, h, 2))
+            units.append(("x", c, h, 3))
 
     with ExitStack() as ctx:
         raw_pool = ctx.enter_context(tc.tile_pool(name="raw", bufs=1))
         grp_pool = ctx.enter_context(tc.tile_pool(name="grp", bufs=GRP_BUFS))
         mx_pool = ctx.enter_context(tc.tile_pool(name="mx", bufs=1))
-        res_pool = ctx.enter_context(tc.tile_pool(name="res", bufs=N_M * N_S))
+        res_pool = ctx.enter_context(tc.tile_pool(name="res", bufs=1))
         psum = ctx.enter_context(tc.psum_pool(name="acc", bufs=8))
+        if PINNED:
+            ctx.enter_context(tc.manual_schedule())
 
         raws = {}
         codes = {}
@@ -54,23 +63,25 @@ def tile_fftmlp_kernel(tc, x, filters_real, filters_imag, grad_out, out):
         for u in units:
             kind, c, h, s = u
             label = "%s%d%d%d" % u
-            raw = raw_pool.tile([P, PACK, W], BF16, name="raw" + label)
             if kind == "g":
-                src = gv[c, :, :, h * W:(h + 1) * W]
-            else:
-                src = xv[c, h, :, :, s * W:(s + 1) * W]
-            nc.sync.dma_start(out=raw[:], in_=src)
-            raws[u] = raw
+                raw = raw_pool.tile([P, PACK, W], BF16, name="raw" + label)
+                nc.sync.dma_start(out=raw[:], in_=gv[c, :, :, h * W:(h + 1) * W])
+                raws[u] = raw[:]
+            elif s < 2:
+                raw = raw_pool.tile([P, PACK, W], BF16, name="raw" + label)
+                nc.sync.dma_start(out=raw[:], in_=xv[c, h, :, :, s * W:(s + 1) * W])
+                raws[u] = raw[:]
+            elif s == 2:
+                raw = raw_pool.tile([P, PACK, 2 * W], BF16, name="raw" + label)
+                nc.sync.dma_start(out=raw[:], in_=xv[c, h, :, :, 2 * W:4 * W])
+                raws[u] = raw[:, :, 0:W]
+                raws[("x", c, h, 3)] = raw[:, :, W:2 * W]
 
         def regroup(copy, u, lo, hi):
             copy(
                 out=groups[u][:, lo:hi, :].rearrange("p (q i) t -> p q t i", i=4),
                 in_=raws[u][:, :, lo:hi].rearrange("p t (q i) -> p q t i", i=4),
             )
-
-        def new_group(u):
-            grouped = grp_pool.tile([P, W, PACK], BF16, name="grouped", align_bytes=64)
-            groups[u] = grouped
 
         def quantise(u):
             label = "%s%d%d%d" % u
@@ -86,37 +97,51 @@ def tile_fftmlp_kernel(tc, x, filters_real, filters_imag, grad_out, out):
             scales[u] = scl
 
         for i, u in enumerate(units):
-            new_group(u)
-            if i < N_SHARE:
-                regroup(nc.vector.tensor_copy, u, 0, V_COLS)
-                regroup(nc.scalar.copy, u, V_COLS, W)
-            else:
-                regroup(nc.vector.tensor_copy, u, 0, W)
+            grouped = grp_pool.tile([P, W, PACK], BF16, name="grouped", align_bytes=64)
+            groups[u] = grouped
+            v_cols = V_COLS if i < N_SHARE else V_COLS_LATE
+            regroup(nc.vector.tensor_copy, u, 0, v_cols)
+            if v_cols < W:
+                regroup(nc.scalar.copy, u, v_cols, W)
             quantise(u)
 
-        def mx_pass(acc, m, c, h, s, start, stop):
-            gu = ("g", c, m // 4, 0)
-            xu = ("x", c, h, s)
+        def mx_tile(m, s):
+            acc = psum.tile([P, W], F32, name="acc")
             cols = slice((m % 4) * P, (m % 4 + 1) * P)
-            nc.tensor.matmul_mx(
-                out=acc[:],
-                lhsT=codes[gu][:, cols].bitcast(E5M2X4),
-                lhsT_scale=scales[gu][:, cols],
-                rhs=codes[xu][:].bitcast(E4M3X4),
-                rhs_scale=scales[xu][:],
-                start=start,
-                stop=stop,
-            )
+            for c in range(N_C):
+                gu = ("g", c, m // 4, 0)
+                for h in range(2):
+                    xu = ("x", c, h, s)
+                    nc.tensor.matmul_mx(
+                        out=acc[:],
+                        lhsT=codes[gu][:, cols].bitcast(E5M2X4),
+                        lhsT_scale=scales[gu][:, cols],
+                        rhs=codes[xu][:].bitcast(E4M3X4),
+                        rhs_scale=scales[xu][:],
+                        start=(c == 0 and h == 0),
+                        stop=(c == 1 and h == 1),
+                    )
+            return acc
 
-        def drain(copy, acc, m, s):
-            res = res_pool.tile([P, W], F32, name="res")
-            copy(out=res[:], in_=acc[:])
-            nc.sync.dma_start(out=out[m * P:(m + 1) * P, s * W:(s + 1) * W], in_=res[:])
+        results = {}
 
-        for s in range(N_S):
+        def drain(acc, m, s):
+            pair = s // 2
+            if s % 2 == 0:
+                res = res_pool.tile([P, 2 * W], F32, name="res%d%d" % (m, pair))
+                results[(m, pair)] = res
+            res = results[(m, pair)]
+            half = slice((s % 2) * W, (s % 2 + 1) * W)
+            nc.scalar.copy(out=res[:, half], in_=acc[:])
+            rows = slice(m * P, (m + 1) * P)
+            if m == N_M - 1 and pair == 1:
+                nc.sync.dma_start(out=out[rows, s * W:(s + 1) * W], in_=res[:, half])
+            elif s % 2 == 1:
+                nc.sync.dma_start(out=out[rows, pair * 2 * W:(pair + 1) * 2 * W], in_=res[:])
+
+        for s in range(2):
             for m in range(N_M):
-                acc = psum.tile([P, W], F32, name="acc")
-                for c in range(N_C):
-                    for h in range(2):
-                        mx_pass(acc, m, c, h, s, c == 0 and h == 0, c == 1 and h == 1)
-                drain(nc.scalar.copy, acc, m, s)
+                drain(mx_tile(m, s), m, s)
+        for m in range(N_M):
+            for s in range(2, 4):
+                drain(mx_tile(m, s), m, s)

@@ -23,6 +23,8 @@ V_COLS_LATE = 512
 N_SHARE = 12
 GRP_BUFS = 6
 PINNED = False
+LHS_PAD = 48
+SLOT = 256
 
 FLOPS = 2 * 2 * TOKENS * OUTF * FEAT
 BYTES = 2 * TOKENS * 2 * FEAT + 2 * TOKENS * OUTF + 4 * OUTF * FEAT
@@ -85,14 +87,20 @@ def tile_fftmlp_kernel(tc, x, filters_real, filters_imag, grad_out, out):
 
         def quantise(u):
             label = "%s%d%d%d" % u
-            cod = mx_pool.tile([P, W], U32, name="cod" + label, align_bytes=64)
-            scl = mx_pool.tile([P, W], U8, name="scl" + label, align_bytes=64)
-            fmt = E5M2X4 if u[0] == "g" else E4M3X4
-            nc.vector.quantize_mx(
-                out=cod[:].bitcast(fmt),
-                scales=scl[:],
-                in_=groups[u][:].rearrange("p w t -> p (w t)"),
-            )
+            flat = groups[u][:].rearrange("p w t -> p (w t)")
+            if u[0] == "g":
+                cod = mx_pool.tile([P, LHS_PAD + W], U32, name="cod" + label, align_bytes=256)
+                scl = mx_pool.tile([P, 4 * SLOT], U8, name="scl" + label, align_bytes=256)
+                for q in range(4):
+                    nc.vector.quantize_mx(
+                        out=cod[:, LHS_PAD + q * P:LHS_PAD + (q + 1) * P].bitcast(E5M2X4),
+                        scales=scl[:, q * SLOT:q * SLOT + P],
+                        in_=flat[:, q * P * PACK:(q + 1) * P * PACK],
+                    )
+            else:
+                cod = mx_pool.tile([P, W], U32, name="cod" + label, align_bytes=256)
+                scl = mx_pool.tile([P, W], U8, name="scl" + label, align_bytes=256)
+                nc.vector.quantize_mx(out=cod[:].bitcast(E4M3X4), scales=scl[:], in_=flat)
             codes[u] = cod
             scales[u] = scl
 
@@ -107,15 +115,15 @@ def tile_fftmlp_kernel(tc, x, filters_real, filters_imag, grad_out, out):
 
         def mx_tile(m, s):
             acc = psum.tile([P, W], F32, name="acc")
-            cols = slice((m % 4) * P, (m % 4 + 1) * P)
+            q = m % 4
             for c in range(N_C):
                 gu = ("g", c, m // 4, 0)
                 for h in range(2):
                     xu = ("x", c, h, s)
                     nc.tensor.matmul_mx(
                         out=acc[:],
-                        lhsT=codes[gu][:, cols].bitcast(E5M2X4),
-                        lhsT_scale=scales[gu][:, cols],
+                        lhsT=codes[gu][:, LHS_PAD + q * P:LHS_PAD + (q + 1) * P].bitcast(E5M2X4),
+                        lhsT_scale=scales[gu][:, q * SLOT:q * SLOT + P],
                         rhs=codes[xu][:].bitcast(E4M3X4),
                         rhs_scale=scales[xu][:],
                         start=(c == 0 and h == 0),

@@ -20,11 +20,9 @@ N_S = FEAT // W
 N_M = OUTF // P
 V_COLS = 320
 V_COLS_LATE = 512
-N_SHARE = 12
+N_SHARE = 8
 GRP_BUFS = 6
 PINNED = False
-LHS_PAD = 48
-SLOT = 256
 
 FLOPS = 2 * 2 * TOKENS * OUTF * FEAT
 BYTES = 2 * TOKENS * 2 * FEAT + 2 * TOKENS * OUTF + 4 * OUTF * FEAT
@@ -43,10 +41,12 @@ def tile_fftmlp_kernel(tc, x, filters_real, filters_imag, grad_out, out):
     for c in range(N_C):
         for h in range(2):
             units.append(("x", c, h, 1))
-    for c in range(N_C):
+    for h in range(2):
+        units.append(("x", 0, h, 2))
+        units.append(("x", 0, h, 3))
+    for s in range(2, 4):
         for h in range(2):
-            units.append(("x", c, h, 2))
-            units.append(("x", c, h, 3))
+            units.append(("x", 1, h, s))
 
     with ExitStack() as ctx:
         raw_pool = ctx.enter_context(tc.tile_pool(name="raw", bufs=1))
@@ -87,20 +87,14 @@ def tile_fftmlp_kernel(tc, x, filters_real, filters_imag, grad_out, out):
 
         def quantise(u):
             label = "%s%d%d%d" % u
-            flat = groups[u][:].rearrange("p w t -> p (w t)")
-            if u[0] == "g":
-                cod = mx_pool.tile([P, LHS_PAD + W], U32, name="cod" + label, align_bytes=256)
-                scl = mx_pool.tile([P, 4 * SLOT], U8, name="scl" + label, align_bytes=256)
-                for q in range(4):
-                    nc.vector.quantize_mx(
-                        out=cod[:, LHS_PAD + q * P:LHS_PAD + (q + 1) * P].bitcast(E5M2X4),
-                        scales=scl[:, q * SLOT:q * SLOT + P],
-                        in_=flat[:, q * P * PACK:(q + 1) * P * PACK],
-                    )
-            else:
-                cod = mx_pool.tile([P, W], U32, name="cod" + label, align_bytes=256)
-                scl = mx_pool.tile([P, W], U8, name="scl" + label, align_bytes=256)
-                nc.vector.quantize_mx(out=cod[:].bitcast(E4M3X4), scales=scl[:], in_=flat)
+            cod = mx_pool.tile([P, W], U32, name="cod" + label, align_bytes=64)
+            scl = mx_pool.tile([P, W], U8, name="scl" + label, align_bytes=64)
+            fmt = E5M2X4 if u[0] == "g" else E4M3X4
+            nc.vector.quantize_mx(
+                out=cod[:].bitcast(fmt),
+                scales=scl[:],
+                in_=groups[u][:].rearrange("p w t -> p (w t)"),
+            )
             codes[u] = cod
             scales[u] = scl
 
@@ -115,15 +109,15 @@ def tile_fftmlp_kernel(tc, x, filters_real, filters_imag, grad_out, out):
 
         def mx_tile(m, s):
             acc = psum.tile([P, W], F32, name="acc")
-            q = m % 4
+            cols = slice((m % 4) * P, (m % 4 + 1) * P)
             for c in range(N_C):
                 gu = ("g", c, m // 4, 0)
                 for h in range(2):
                     xu = ("x", c, h, s)
                     nc.tensor.matmul_mx(
                         out=acc[:],
-                        lhsT=codes[gu][:, LHS_PAD + q * P:LHS_PAD + (q + 1) * P].bitcast(E5M2X4),
-                        lhsT_scale=scales[gu][:, q * SLOT:q * SLOT + P],
+                        lhsT=codes[gu][:, cols].bitcast(E5M2X4),
+                        lhsT_scale=scales[gu][:, cols],
                         rhs=codes[xu][:].bitcast(E4M3X4),
                         rhs_scale=scales[xu][:],
                         start=(c == 0 and h == 0),
@@ -134,22 +128,20 @@ def tile_fftmlp_kernel(tc, x, filters_real, filters_imag, grad_out, out):
         results = {}
 
         def drain(acc, m, s):
-            pair = s // 2
-            if s % 2 == 0:
-                res = res_pool.tile([P, 2 * W], F32, name="res%d%d" % (m, pair))
-                results[(m, pair)] = res
-            res = results[(m, pair)]
-            half = slice((s % 2) * W, (s % 2 + 1) * W)
-            nc.scalar.copy(out=res[:, half], in_=acc[:])
             rows = slice(m * P, (m + 1) * P)
-            if m == N_M - 1 and pair == 1:
-                nc.sync.dma_start(out=out[rows, s * W:(s + 1) * W], in_=res[:, half])
-            elif s % 2 == 1:
-                nc.sync.dma_start(out=out[rows, pair * 2 * W:(pair + 1) * 2 * W], in_=res[:])
+            if s >= 2:
+                res = res_pool.tile([P, W], F32, name="res%d%d" % (m, s))
+                nc.scalar.copy(out=res[:], in_=acc[:])
+                nc.sync.dma_start(out=out[rows, s * W:(s + 1) * W], in_=res[:])
+                return
+            if s == 0:
+                res = res_pool.tile([P, 2 * W], F32, name="res%d" % m)
+                results[m] = res
+            res = results[m]
+            nc.scalar.copy(out=res[:, s * W:(s + 1) * W], in_=acc[:])
+            if s == 1:
+                nc.sync.dma_start(out=out[rows, 0:2 * W], in_=res[:])
 
-        for s in range(2):
+        for s in range(N_S):
             for m in range(N_M):
-                drain(mx_tile(m, s), m, s)
-        for m in range(N_M):
-            for s in range(2, 4):
                 drain(mx_tile(m, s), m, s)

@@ -22,7 +22,6 @@ V_COLS = 320
 V_COLS_LATE = 512
 N_SHARE = 8
 GRP_BUFS = 6
-PINNED = False
 
 FLOPS = 2 * 2 * TOKENS * OUTF * FEAT
 BYTES = 2 * TOKENS * 2 * FEAT + 2 * TOKENS * OUTF + 4 * OUTF * FEAT
@@ -54,8 +53,7 @@ def tile_fftmlp_kernel(tc, x, filters_real, filters_imag, grad_out, out):
         mx_pool = ctx.enter_context(tc.tile_pool(name="mx", bufs=1))
         res_pool = ctx.enter_context(tc.tile_pool(name="res", bufs=1))
         psum = ctx.enter_context(tc.psum_pool(name="acc", bufs=8))
-        if PINNED:
-            ctx.enter_context(tc.manual_schedule())
+        ctx.enter_context(tc.manual_schedule(engines={mybir.EngineType.DVE}))
 
         raws = {}
         codes = {}
@@ -105,7 +103,9 @@ def tile_fftmlp_kernel(tc, x, filters_real, filters_imag, grad_out, out):
             regroup(nc.vector.tensor_copy, u, 0, v_cols)
             if v_cols < W:
                 regroup(nc.scalar.copy, u, v_cols, W)
-            quantise(u)
+            if i > 0:
+                quantise(units[i - 1])
+        quantise(units[-1])
 
         def mx_tile(m, s):
             acc = psum.tile([P, W], F32, name="acc")

@@ -102,10 +102,13 @@ def tile_fftmlp_kernel(tc, x, filters_real, filters_imag, grad_out, out):
             v_cols = V_COLS if i < N_SHARE else V_COLS_LATE
             regroup(nc.vector.tensor_copy, u, 0, v_cols)
             if v_cols < W:
-                regroup(nc.scalar.copy, u, v_cols, W)
-            if i > 0:
+                nc.scalar.copy(
+                    out=groups[u][:, v_cols:W, :],
+                    in_=raws[u][:, :, v_cols:W].rearrange("p t w -> p w t"),
+                )
+            if i % 2 == 1:
                 quantise(units[i - 1])
-        quantise(units[-1])
+                quantise(u)
 
         def mx_tile(m, s):
             acc = psum.tile([P, W], F32, name="acc")

@@ -79,8 +79,8 @@ def tile_fftmlp_kernel(tc, x, filters_real, filters_imag, grad_out, out):
 
         def regroup(copy, u, lo, hi):
             copy(
-                out=groups[u][:, lo:hi, :].rearrange("p (q i) t -> p q t i", i=4),
-                in_=raws[u][:, :, lo:hi].rearrange("p t (q i) -> p q t i", i=4),
+                out=groups[u][:, lo:hi, :].rearrange("p (q i) t -> p q t i", i=8),
+                in_=raws[u][:, :, lo:hi].rearrange("p t (q i) -> p q t i", i=8),
             )
 
         def quantise(u):

from contextlib import ExitStack

import concourse.mybir as mybir

BF16 = mybir.dt.bfloat16
F32 = mybir.dt.float32
U32 = mybir.dt.uint32
U8 = mybir.dt.uint8
E4M3X4 = mybir.dt.float8_e4m3fn_x4
E5M2X4 = mybir.dt.float8_e5m2_x4

P = 128
PACK = 4
TOKENS = 1024
FEAT = 2048
OUTF = 1024
W = 512
N_C = TOKENS // (P * PACK)
N_S = FEAT // W
N_M = OUTF // P
V_COLS = 320
V_COLS_LATE = 512
N_SHARE = 8
GRP_BUFS = 6

FLOPS = 2 * 2 * TOKENS * OUTF * FEAT
BYTES = 2 * TOKENS * 2 * FEAT + 2 * TOKENS * OUTF + 4 * OUTF * FEAT


def tile_fftmlp_kernel(tc, x, filters_real, filters_imag, grad_out, out):
    nc = tc.nc
    xv = x.rearrange("(c p j) h f -> c h p j f", c=N_C, p=P, j=PACK)
    gv = grad_out.rearrange("(c p j) o -> c p j o", c=N_C, p=P, j=PACK)

    units = []
    for c in range(N_C):
        for h in range(2):
            units.append(("g", c, h, 0))
            units.append(("x", c, h, 0))
    for c in range(N_C):
        for h in range(2):
            units.append(("x", c, h, 1))
    for h in range(2):
        units.append(("x", 0, h, 2))
        units.append(("x", 0, h, 3))
    for s in range(2, 4):
        for h in range(2):
            units.append(("x", 1, h, s))

    with ExitStack() as ctx:
        raw_pool = ctx.enter_context(tc.tile_pool(name="raw", bufs=1))
        grp_pool = ctx.enter_context(tc.tile_pool(name="grp", bufs=GRP_BUFS))
        mx_pool = ctx.enter_context(tc.tile_pool(name="mx", bufs=1))
        res_pool = ctx.enter_context(tc.tile_pool(name="res", bufs=1))
        psum = ctx.enter_context(tc.psum_pool(name="acc", bufs=8))
        ctx.enter_context(tc.manual_schedule(engines={mybir.EngineType.DVE}))

        raws = {}
        codes = {}
        scales = {}
        groups = {}

        for u in units:
            kind, c, h, s = u
            label = "%s%d%d%d" % u
            if kind == "g":
                raw = raw_pool.tile([P, PACK, W], BF16, name="raw" + label)
                nc.sync.dma_start(out=raw[:], in_=gv[c, :, :, h * W:(h + 1) * W])
                raws[u] = raw[:]
            elif s < 2:
                raw = raw_pool.tile([P, PACK, W], BF16, name="raw" + label)
                nc.sync.dma_start(out=raw[:], in_=xv[c, h, :, :, s * W:(s + 1) * W])
                raws[u] = raw[:]
            elif s == 2:
                raw = raw_pool.tile([P, PACK, 2 * W], BF16, name="raw" + label)
                nc.sync.dma_start(out=raw[:], in_=xv[c, h, :, :, 2 * W:4 * W])
                raws[u] = raw[:, :, 0:W]
                raws[("x", c, h, 3)] = raw[:, :, W:2 * W]

        def regroup(copy, u, lo, hi):
            copy(
                out=groups[u][:, lo:hi, :].rearrange("p (q i) t -> p q t i", i=8),
                in_=raws[u][:, :, lo:hi].rearrange("p t (q i) -> p q t i", i=8),
            )

        def quantise(u):
            label = "%s%d%d%d" % u
            cod = mx_pool.tile([P, W], U32, name="cod" + label, align_bytes=64)
            scl = mx_pool.tile([P, W], U8, name="scl" + label, align_bytes=64)
            fmt = E5M2X4 if u[0] == "g" else E4M3X4
            nc.vector.quantize_mx(
                out=cod[:].bitcast(fmt),
                scales=scl[:],
                in_=groups[u][:].rearrange("p w t -> p (w t)"),
            )
            codes[u] = cod
            scales[u] = scl

        for i, u in enumerate(units):
            grouped = grp_pool.tile([P, W, PACK], BF16, name="grouped", align_bytes=64)
            groups[u] = grouped
            v_cols = V_COLS if i < N_SHARE else V_COLS_LATE
            regroup(nc.vector.tensor_copy, u, 0, v_cols)
            if v_cols < W:
                nc.scalar.copy(
                    out=groups[u][:, v_cols:W, :],
                    in_=raws[u][:, :, v_cols:W].rearrange("p t w -> p w t"),
                )
            if i % 2 == 1:
                quantise(units[i - 1])
                quantise(u)

        def mx_tile(m, s):
            acc = psum.tile([P, W], F32, name="acc")
            cols = slice((m % 4) * P, (m % 4 + 1) * P)
            for c in range(N_C):
                gu = ("g", c, m // 4, 0)
                for h in range(2):
                    xu = ("x", c, h, s)
                    nc.tensor.matmul_mx(
                        out=acc[:],
                        lhsT=codes[gu][:, cols].bitcast(E5M2X4),
                        lhsT_scale=scales[gu][:, cols],
                        rhs=codes[xu][:].bitcast(E4M3X4),
                        rhs_scale=scales[xu][:],
                        start=(c == 0 and h == 0),
                        stop=(c == 1 and h == 1),
                    )
            return acc

        results = {}

        def drain(acc, m, s):
            rows = slice(m * P, (m + 1) * P)
            if s >= 2:
                res = res_pool.tile([P, W], F32, name="res%d%d" % (m, s))
                nc.scalar.copy(out=res[:], in_=acc[:])
                nc.sync.dma_start(out=out[rows, s * W:(s + 1) * W], in_=res[:])
                return
            if s == 0:
                res = res_pool.tile([P, 2 * W], F32, name="res%d" % m)
                results[m] = res
            res = results[m]
            nc.scalar.copy(out=res[:, s * W:(s + 1) * W], in_=acc[:])
            if s == 1:
                nc.sync.dma_start(out=out[rows, 0:2 * W], in_=res[:])

        for s in range(N_S):
            for m in range(N_M):
                drain(mx_tile(m, s), m, s)
